import numpy as np
import ml_dtypes


def mxq(x, axis, fmt="e4m3"):
    dtype, down = {"e4m3": (ml_dtypes.float8_e4m3fn, 7), "e5m2": (ml_dtypes.float8_e5m2, 14)}[fmt]
    v = np.moveaxis(np.asarray(x, np.float32).astype(ml_dtypes.bfloat16).astype(np.float64), axis, -1)
    blocks = v.reshape(v.shape[:-1] + (-1, 32))
    amax = np.abs(blocks).max(-1, keepdims=True)
    byte = np.maximum(np.where(amax > 0, np.frexp(amax)[1] - 1 + 127, 0) - down, 1)
    scale = np.exp2(byte - 127.0)
    codes = (blocks / scale).astype(np.float32).astype(dtype).astype(np.float64)
    return np.moveaxis((codes * scale).reshape(v.shape), -1, axis)


WIDE = False


def mx_kscale(k):
    if not WIDE:
        return np.ones(k)
    levels = np.array([10, -10, 5, -5, 0])
    a = np.random.permutation(np.resize(levels, k // 512 * 4)).reshape(k // 512, 4)
    idx = np.arange(k)
    return np.exp2(a[idx // 512, idx % 128 // 32])


BF16 = ml_dtypes.bfloat16


def bf(x):
    return np.asarray(x, np.float32).astype(BF16)


def f64(x):
    return np.asarray(x).astype(np.float64)


B, S, N, D = 4, 128, 16384, 512


def setup_inputs():
    s = mx_kscale(N)
    return {"input_numeric": bf(np.random.standard_normal((B, S, 1))),
            "proj_w": bf(np.random.standard_normal((N, 1))),
            "proj_b": bf(np.random.standard_normal(N) + np.log(s)),
            "emb_table": bf(np.random.standard_normal((N, D)) * 0.15 * np.sqrt(N) * np.mean(s) / s[:, None])}


def reference(input_numeric, proj_w, proj_b, emb_table):
    logits = f64(input_numeric) * f64(proj_w)[:, 0] + f64(proj_b)
    e = np.exp(logits - logits.max(-1, keepdims=True))
    weights = e / e.sum(-1, keepdims=True)
    return mxq(weights, 2, "e4m3") @ mxq(f64(emb_table), 0, "e4m3")

@@ -1,0 +1,200 @@
+from contextlib import ExitStack
+
+import concourse.mybir as mybir
+from concourse.masks import make_identity
+
+F32 = mybir.dt.float32
+BF16 = mybir.dt.bfloat16
+U32 = mybir.dt.uint32
+U8 = mybir.dt.uint8
+FP8X4 = mybir.dt.float8_e4m3fn_x4
+ALU = mybir.AluOpType
+ACT = mybir.ActivationFunctionType
+AXIS = mybir.AxisListType
+
+P = 128
+BATCHES = 4
+VOCAB = 16384
+DIM = 512
+PACK = 4
+K_PASS = P * PACK
+PASSES = VOCAB // K_PASS
+CHUNK = 2048
+CHUNKS = VOCAB // CHUNK
+CHUNK_PASSES = CHUNK // K_PASS
+PLANES = 4
+EXP_BUFS = CHUNKS + 1
+TABLE_LOADS = 4
+
+FLOPS = 2 * BATCHES * P * VOCAB * DIM
+
+
+def tile_softembedding_k_kernel(tc, input_numeric, proj_w, proj_b, emb_table, out):
+    nc = tc.nc
+    with ExitStack() as ctx:
+        keep = ctx.enter_context(tc.tile_pool(name="keep", bufs=1))
+        exp_pool = ctx.enter_context(tc.tile_pool(name="exp_pool", bufs=EXP_BUFS))
+        stats = ctx.enter_context(tc.tile_pool(name="stats", bufs=2))
+        psum_turn = ctx.enter_context(tc.psum_pool(name="psum_turn", bufs=4))
+        psum_out = ctx.enter_context(tc.psum_pool(name="psum_out", bufs=2))
+
+        identity = keep.tile([P, P], F32)
+        make_identity(nc, identity[:])
+
+        x_bf = keep.tile([P, BATCHES], BF16)
+        with nc.allow_non_contiguous_dma(reason="512 scalars, one token to a partition"):
+            nc.sync.dma_start(out=x_bf[:], in_=input_numeric.rearrange("b s o -> s (b o)"))
+        x_col = keep.tile([P, BATCHES], F32)
+        nc.vector.tensor_copy(out=x_col[:], in_=x_bf[:])
+
+        w_all = keep.tile([P, VOCAB], BF16)
+        b_all = keep.tile([P, VOCAB], BF16)
+        w_vector = proj_w.rearrange("n o -> (n o)")
+
+        table_codes = keep.tile([P, PASSES, DIM], U32, align_bytes=64)
+        table_scales = keep.tile([P, PASSES // PLANES, DIM], U8, align_bytes=64)
+
+        def table_plane(g):
+            return table_scales[4 * (g % PLANES) : P, g // PLANES, :]
+
+        def load_projection(j):
+            cols = slice(j * CHUNK, (j + 1) * CHUNK)
+            nc.sync.dma_start(out=w_all[:, cols], in_=w_vector[cols].partition_broadcast(P))
+            nc.sync.dma_start(out=b_all[:, cols], in_=proj_b[cols].partition_broadcast(P))
+
+        def quantise_table_pass(stage, g):
+            table_rows = stage.tile([P, PACK, DIM], BF16, bufs=TABLE_LOADS)
+            nc.sync.dma_start(
+                out=table_rows[:].rearrange("p (u e) d -> p u (e d)", u=2),
+                in_=emb_table[g * K_PASS : (g + 1) * K_PASS, :].rearrange(
+                    "(u p e) d -> p u (e d)", u=2, e=2
+                ),
+            )
+            table_grouped = stage.tile([P, DIM, PACK], BF16, align_bytes=64)
+            dst = table_grouped[:].rearrange("p (c i) t -> p c t i", i=4)
+            src = table_rows[:].rearrange("p t (c i) -> p c t i", i=4)
+            if g % 3 == 0:
+                nc.vector.tensor_copy(out=dst, in_=src)
+            else:
+                nc.scalar.copy(out=dst, in_=src)
+            nc.vector.quantize_mx(
+                out=table_codes[:, g, :].bitcast(FP8X4),
+                scales=table_plane(g),
+                in_=table_grouped[:].rearrange("p d t -> p (d t)"),
+            )
+
+        def softmax_chunk(b, j, neg_max, part_sum):
+            cols = slice(j * CHUNK, (j + 1) * CHUNK)
+            exps = exp_pool.tile([P, CHUNK], F32)
+            nc.vector.scalar_tensor_tensor(
+                out=exps[:],
+                in0=w_all[:, cols],
+                scalar=x_col[:, b : b + 1],
+                in1=b_all[:, cols],
+                op0=ALU.mult,
+                op1=ALU.add,
+            )
+            nc.vector.tensor_reduce(
+                out=neg_max[:, j : j + 1], in_=exps[:], axis=AXIS.X, op=ALU.max, negate=True
+            )
+            nc.scalar.activation(
+                out=exps[:],
+                in_=exps[:],
+                func=ACT.Exp,
+                bias=neg_max[:, j : j + 1],
+                scale=1.0,
+                accum_out=part_sum[:, j : j + 1],
+            )
+            return exps
+
+        def softmax_scales(neg_max, part_sum):
+            neg_top = stats.tile([P, 1], F32)
+            nc.vector.tensor_reduce(out=neg_top[:], in_=neg_max[:], axis=AXIS.X, op=ALU.min)
+            factor = stats.tile([P, CHUNKS], F32)
+            nc.scalar.activation(
+                out=factor[:], in_=neg_max[:], func=ACT.Exp, bias=neg_top[:, 0:1], scale=-1.0
+            )
+            weighted = stats.tile([P, CHUNKS], F32)
+            nc.vector.tensor_tensor(out=weighted[:], in0=factor[:], in1=part_sum[:], op=ALU.mult)
+            total = stats.tile([P, 1], F32)
+            nc.vector.tensor_reduce(out=total[:], in_=weighted[:], axis=AXIS.X, op=ALU.add)
+            inv_total = stats.tile([P, 1], F32)
+            nc.vector.reciprocal(out=inv_total[:], in_=total[:])
+            chunk_scale = stats.tile([P, CHUNKS], F32)
+            nc.vector.tensor_scalar(
+                out=chunk_scale[:], in0=factor[:], scalar1=inv_total[:, 0:1], scalar2=None, op0=ALU.mult
+            )
+            return chunk_scale
+
+        def weights_chunk(stage, j, exps, chunk_scale, acc, vector_is_busy):
+            weight_rows = stage.tile([P, CHUNK], BF16)
+            if j % 4 == 0 or not vector_is_busy:
+                nc.vector.tensor_scalar(
+                    out=weight_rows[:], in0=exps[:], scalar1=chunk_scale[:, j : j + 1], scalar2=None, op0=ALU.mult
+                )
+            else:
+                nc.scalar.activation(
+                    out=weight_rows[:], in_=exps[:], func=ACT.Copy, scale=chunk_scale[:, j : j + 1]
+                )
+            words = weight_rows[:].bitcast(F32)
+            weight_grouped = stage.tile([P, CHUNK_PASSES, P, PACK], BF16, align_bytes=64)
+            grouped_words = weight_grouped[:].bitcast(F32)
+            for half in range(CHUNK_PASSES // 2):
+                turned = psum_turn.tile([P, 2, 2, P], F32)
+                for c in range(2):
+                    for u in range(2):
+                        first = ((2 * half + c) * 2 + u) * P
+                        nc.tensor.transpose(turned[:, c, u, :], words[:, first : first + P], identity[:])
+                nc.scalar.copy(
+                    out=grouped_words[:, 2 * half : 2 * half + 2, :, :],
+                    in_=turned[:].rearrange("p c u m -> p c m u"),
+                )
+            weight_codes = stage.tile([P, CHUNK_PASSES * P], U32, align_bytes=64)
+            weight_scales = stage.tile([P, CHUNK_PASSES * P], U8, align_bytes=64)
+            nc.vector.quantize_mx(
+                out=weight_codes[:].bitcast(FP8X4),
+                scales=weight_scales[:],
+                in_=weight_grouped[:].rearrange("p c m t -> p (c m t)"),
+            )
+            for c in range(CHUNK_PASSES):
+                g = j * CHUNK_PASSES + c
+                tokens = slice(c * P, (c + 1) * P)
+                nc.tensor.matmul_mx(
+                    out=acc[:],
+                    lhsT=weight_codes[:, tokens].bitcast(FP8X4),
+                    lhsT_scale=weight_scales[:, tokens],
+                    rhs=table_codes[:, g, :].bitcast(FP8X4),
+                    rhs_scale=table_plane(g),
+                    start=(g == 0),
+                    stop=(g == PASSES - 1),
+                )
+
+        neg_max = stats.tile([P, CHUNKS], F32)
+        part_sum = stats.tile([P, CHUNKS], F32)
+        row_exps = []
+        with tc.tile_pool(name="table_stage", bufs=2) as table_stage:
+            for j in range(CHUNKS):
+                load_projection(j)
+                row_exps.append(softmax_chunk(0, j, neg_max, part_sum))
+                for g in range(j * CHUNK_PASSES, (j + 1) * CHUNK_PASSES):
+                    quantise_table_pass(table_stage, g)
+        chunk_scale = softmax_scales(neg_max, part_sum)
+
+        with tc.tile_pool(name="weight_stage", bufs=2, reuse_waits="tile") as weight_stage:
+            for b in range(BATCHES):
+                acc = psum_out.tile([P, DIM], F32)
+                more = b + 1 < BATCHES
+                next_exps = []
+                if more:
+                    neg_max = stats.tile([P, CHUNKS], F32)
+                    part_sum = stats.tile([P, CHUNKS], F32)
+                for j in range(CHUNKS):
+                    if more:
+                        next_exps.append(softmax_chunk(b + 1, j, neg_max, part_sum))
+                    weights_chunk(weight_stage, j, row_exps[j], chunk_scale, acc, more)
+                result = weight_stage.tile([P, DIM], F32)
+                nc.scalar.copy(out=result[:], in_=acc[:])
+                nc.sync.dma_start(out=out[b], in_=result[:])
+                if more:
+                    chunk_scale = softmax_scales(neg_max, part_sum)
+                row_exps = next_exps

@@ -24,7 +24,9 @@ CHUNKS = VOCAB // CHUNK
 CHUNK_PASSES = CHUNK // K_PASS
 PLANES = 4
 EXP_BUFS = CHUNKS + 1
-TABLE_LOADS = 4
+TOTAL = BATCHES * CHUNKS
+TABLE_AHEAD = 3
+TABLE_LAG = 2
 
 FLOPS = 2 * BATCHES * P * VOCAB * DIM
 
@@ -32,6 +34,7 @@ FLOPS = 2 * BATCHES * P * VOCAB * DIM
 def tile_softembedding_k_kernel(tc, input_numeric, proj_w, proj_b, emb_table, out):
     nc = tc.nc
     with ExitStack() as ctx:
+        ctx.enter_context(tc.manual_schedule())
         keep = ctx.enter_context(tc.tile_pool(name="keep", bufs=1))
         exp_pool = ctx.enter_context(tc.tile_pool(name="exp_pool", bufs=EXP_BUFS))
         stats = ctx.enter_context(tc.tile_pool(name="stats", bufs=2))
@@ -62,32 +65,53 @@ def tile_softembedding_k_kernel(tc, input_numeric, proj_w, proj_b, emb_table, ou
             nc.sync.dma_start(out=w_all[:, cols], in_=w_vector[cols].partition_broadcast(P))
             nc.sync.dma_start(out=b_all[:, cols], in_=proj_b[cols].partition_broadcast(P))
 
-        def quantise_table_pass(stage, g):
-            table_rows = stage.tile([P, PACK, DIM], BF16, bufs=TABLE_LOADS)
+        table_rows = {}
+        table_grouped = {}
+
+        def load_table(stage, g):
+            rows = stage.tile([P, PACK, DIM], BF16, bufs=TABLE_AHEAD + 1)
             nc.sync.dma_start(
-                out=table_rows[:].rearrange("p (u e) d -> p u (e d)", u=2),
+                out=rows[:].rearrange("p (u e) d -> p u (e d)", u=2),
                 in_=emb_table[g * K_PASS : (g + 1) * K_PASS, :].rearrange(
                     "(u p e) d -> p u (e d)", u=2, e=2
                 ),
             )
-            table_grouped = stage.tile([P, DIM, PACK], BF16, align_bytes=64)
-            dst = table_grouped[:].rearrange("p (c i) t -> p c t i", i=4)
-            src = table_rows[:].rearrange("p t (c i) -> p c t i", i=4)
+            table_rows[g] = rows
+
+        def regroup_table(stage, g):
+            grouped = stage.tile([P, DIM, PACK], BF16, align_bytes=64, bufs=TABLE_LAG + 1)
+            dst = grouped[:].rearrange("p (c i) t -> p c t i", i=4)
+            src = table_rows[g][:].rearrange("p t (c i) -> p c t i", i=4)
             if g % 3 == 0:
                 nc.vector.tensor_copy(out=dst, in_=src)
             else:
                 nc.scalar.copy(out=dst, in_=src)
+            table_grouped[g] = grouped
+
+        def quantise_table(g):
             nc.vector.quantize_mx(
                 out=table_codes[:, g, :].bitcast(FP8X4),
                 scales=table_plane(g),
-                in_=table_grouped[:].rearrange("p d t -> p (d t)"),
+                in_=table_grouped[g][:].rearrange("p d t -> p (d t)"),
             )
 
-        def softmax_chunk(b, j, neg_max, part_sum):
+        exps = {}
+        neg_max = {}
+        part_sum = {}
+        neg_top = {}
+        chunk_scale = {}
+
+        def logits(k):
+            b, j = divmod(k, CHUNKS)
+            if j == 0:
+                row_neg_max = stats.tile([P, CHUNKS], F32)
+                row_part_sum = stats.tile([P, CHUNKS], F32)
+                neg_max[b] = row_neg_max
+                part_sum[b] = row_part_sum
             cols = slice(j * CHUNK, (j + 1) * CHUNK)
-            exps = exp_pool.tile([P, CHUNK], F32)
+            chunk = exp_pool.tile([P, CHUNK], F32)
             nc.vector.scalar_tensor_tensor(
-                out=exps[:],
+                out=chunk[:],
                 in0=w_all[:, cols],
                 scalar=x_col[:, b : b + 1],
                 in1=b_all[:, cols],
@@ -95,106 +119,159 @@ def tile_softembedding_k_kernel(tc, input_numeric, proj_w, proj_b, emb_table, ou
                 op1=ALU.add,
             )
             nc.vector.tensor_reduce(
-                out=neg_max[:, j : j + 1], in_=exps[:], axis=AXIS.X, op=ALU.max, negate=True
+                out=neg_max[b][:, j : j + 1], in_=chunk[:], axis=AXIS.X, op=ALU.max, negate=True
             )
-            nc.scalar.activation(
-                out=exps[:],
-                in_=exps[:],
-                func=ACT.Exp,
-                bias=neg_max[:, j : j + 1],
-                scale=1.0,
-                accum_out=part_sum[:, j : j + 1],
-            )
-            return exps
+            exps[k] = chunk
 
-        def softmax_scales(neg_max, part_sum):
-            neg_top = stats.tile([P, 1], F32)
-            nc.vector.tensor_reduce(out=neg_top[:], in_=neg_max[:], axis=AXIS.X, op=ALU.min)
+        def exponentials(k):
+            b, j = divmod(k, CHUNKS)
+            nc.scalar.activation(
+                out=exps[k][:],
+                in_=exps[k][:],
+                func=ACT.Exp,
+                bias=neg_max[b][:, j : j + 1],
+                scale=1.0,
+                accum_out=part_sum[b][:, j : j + 1],
+            )
+
+        def row_top(b):
+            top = stats.tile([P, 1], F32)
+            nc.vector.tensor_reduce(out=top[:], in_=neg_max[b][:], axis=AXIS.X, op=ALU.min)
+            neg_top[b] = top
+
+        def row_scales(b):
             factor = stats.tile([P, CHUNKS], F32)
             nc.scalar.activation(
-                out=factor[:], in_=neg_max[:], func=ACT.Exp, bias=neg_top[:, 0:1], scale=-1.0
+                out=factor[:], in_=neg_max[b][:], func=ACT.Exp, bias=neg_top[b][:, 0:1], scale=-1.0
             )
             weighted = stats.tile([P, CHUNKS], F32)
-            nc.vector.tensor_tensor(out=weighted[:], in0=factor[:], in1=part_sum[:], op=ALU.mult)
+            nc.vector.tensor_tensor(out=weighted[:], in0=factor[:], in1=part_sum[b][:], op=ALU.mult)
             total = stats.tile([P, 1], F32)
             nc.vector.tensor_reduce(out=total[:], in_=weighted[:], axis=AXIS.X, op=ALU.add)
             inv_total = stats.tile([P, 1], F32)
             nc.vector.reciprocal(out=inv_total[:], in_=total[:])
-            chunk_scale = stats.tile([P, CHUNKS], F32)
+            scales = stats.tile([P, CHUNKS], F32)
             nc.vector.tensor_scalar(
-                out=chunk_scale[:], in0=factor[:], scalar1=inv_total[:, 0:1], scalar2=None, op0=ALU.mult
+                out=scales[:], in0=factor[:], scalar1=inv_total[:, 0:1], scalar2=None, op0=ALU.mult
             )
-            return chunk_scale
+            chunk_scale[b] = scales
 
-        def weights_chunk(stage, j, exps, chunk_scale, acc, vector_is_busy):
-            weight_rows = stage.tile([P, CHUNK], BF16)
-            if j % 4 == 0 or not vector_is_busy:
-                nc.vector.tensor_scalar(
-                    out=weight_rows[:], in0=exps[:], scalar1=chunk_scale[:, j : j + 1], scalar2=None, op0=ALU.mult
+        weight_rows = {}
+        turned = {}
+        weight_grouped = {}
+        weight_codes = {}
+        weight_scales = {}
+        acc = {}
+
+        def normalise(stage, k, on_scalar):
+            b, j = divmod(k, CHUNKS)
+            rows = stage.tile([P, CHUNK], BF16)
+            if on_scalar:
+                nc.scalar.activation(
+                    out=rows[:], in_=exps[k][:], func=ACT.Copy, scale=chunk_scale[b][:, j : j + 1]
                 )
             else:
-                nc.scalar.activation(
-                    out=weight_rows[:], in_=exps[:], func=ACT.Copy, scale=chunk_scale[:, j : j + 1]
+                nc.vector.tensor_scalar(
+                    out=rows[:], in0=exps[k][:], scalar1=chunk_scale[b][:, j : j + 1], scalar2=None, op0=ALU.mult
                 )
-            words = weight_rows[:].bitcast(F32)
-            weight_grouped = stage.tile([P, CHUNK_PASSES, P, PACK], BF16, align_bytes=64)
-            grouped_words = weight_grouped[:].bitcast(F32)
+            weight_rows[k] = rows
+
+        def turn(k):
+            words = weight_rows[k][:].bitcast(F32)
+            turned[k] = []
             for half in range(CHUNK_PASSES // 2):
-                turned = psum_turn.tile([P, 2, 2, P], F32)
+                bank = psum_turn.tile([P, 2, 2, P], F32)
                 for c in range(2):
                     for u in range(2):
                         first = ((2 * half + c) * 2 + u) * P
-                        nc.tensor.transpose(turned[:, c, u, :], words[:, first : first + P], identity[:])
+                        nc.tensor.transpose(bank[:, c, u, :], words[:, first : first + P], identity[:])
+                turned[k].append(bank)
+
+        def regroup(stage, k):
+            grouped = stage.tile([P, CHUNK_PASSES, P, PACK], BF16, align_bytes=64)
+            grouped_words = grouped[:].bitcast(F32)
+            for half in range(CHUNK_PASSES // 2):
                 nc.scalar.copy(
                     out=grouped_words[:, 2 * half : 2 * half + 2, :, :],
-                    in_=turned[:].rearrange("p c u m -> p c m u"),
+                    in_=turned[k][half][:].rearrange("p c u m -> p c m u"),
                 )
-            weight_codes = stage.tile([P, CHUNK_PASSES * P], U32, align_bytes=64)
-            weight_scales = stage.tile([P, CHUNK_PASSES * P], U8, align_bytes=64)
+            weight_grouped[k] = grouped
+
+        def quantise(stage, k):
+            codes = stage.tile([P, CHUNK_PASSES * P], U32, align_bytes=64)
+            scales = stage.tile([P, CHUNK_PASSES * P], U8, align_bytes=64)
             nc.vector.quantize_mx(
-                out=weight_codes[:].bitcast(FP8X4),
-                scales=weight_scales[:],
-                in_=weight_grouped[:].rearrange("p c m t -> p (c m t)"),
+                out=codes[:].bitcast(FP8X4),
+                scales=scales[:],
+                in_=weight_grouped[k][:].rearrange("p c m t -> p (c m t)"),
             )
+            weight_codes[k] = codes
+            weight_scales[k] = scales
+
+        def multiply(k):
+            b, j = divmod(k, CHUNKS)
+            if j == 0:
+                row_acc = psum_out.tile([P, DIM], F32)
+                acc[b] = row_acc
             for c in range(CHUNK_PASSES):
                 g = j * CHUNK_PASSES + c
                 tokens = slice(c * P, (c + 1) * P)
                 nc.tensor.matmul_mx(
-                    out=acc[:],
-                    lhsT=weight_codes[:, tokens].bitcast(FP8X4),
-                    lhsT_scale=weight_scales[:, tokens],
+                    out=acc[b][:],
+                    lhsT=weight_codes[k][:, tokens].bitcast(FP8X4),
+                    lhsT_scale=weight_scales[k][:, tokens],
                     rhs=table_codes[:, g, :].bitcast(FP8X4),
                     rhs_scale=table_plane(g),
                     start=(g == 0),
                     stop=(g == PASSES - 1),
                 )
 
-        neg_max = stats.tile([P, CHUNKS], F32)
-        part_sum = stats.tile([P, CHUNKS], F32)
-        row_exps = []
-        with tc.tile_pool(name="table_stage", bufs=2) as table_stage:
-            for j in range(CHUNKS):
-                load_projection(j)
-                row_exps.append(softmax_chunk(0, j, neg_max, part_sum))
-                for g in range(j * CHUNK_PASSES, (j + 1) * CHUNK_PASSES):
-                    quantise_table_pass(table_stage, g)
-        chunk_scale = softmax_scales(neg_max, part_sum)
+        def store(stage, b):
+            result = stage.tile([P, DIM], F32)
+            nc.scalar.copy(out=result[:], in_=acc[b][:])
+            nc.sync.dma_start(out=out[b], in_=result[:])
+
+        with tc.tile_pool(name="table_stage", bufs=1) as table_stage:
+            load_projection(0)
+            for g in range(TABLE_AHEAD):
+                load_table(table_stage, g)
+            for k in range(CHUNKS):
+                if k + 1 < CHUNKS:
+                    load_projection(k + 1)
+                logits(k)
+                if k >= 1:
+                    exponentials(k - 1)
+                for g in range(k * CHUNK_PASSES, (k + 1) * CHUNK_PASSES):
+                    if g + TABLE_AHEAD < PASSES:
+                        load_table(table_stage, g + TABLE_AHEAD)
+                    regroup_table(table_stage, g)
+                    if g >= TABLE_LAG:
+                        quantise_table(g - TABLE_LAG)
+            for g in range(PASSES - TABLE_LAG, PASSES):
+                quantise_table(g)
 
         with tc.tile_pool(name="weight_stage", bufs=2, reuse_waits="tile") as weight_stage:
-            for b in range(BATCHES):
-                acc = psum_out.tile([P, DIM], F32)
-                more = b + 1 < BATCHES
-                next_exps = []
-                if more:
-                    neg_max = stats.tile([P, CHUNKS], F32)
-                    part_sum = stats.tile([P, CHUNKS], F32)
-                for j in range(CHUNKS):
-                    if more:
-                        next_exps.append(softmax_chunk(b + 1, j, neg_max, part_sum))
-                    weights_chunk(weight_stage, j, row_exps[j], chunk_scale, acc, more)
-                result = weight_stage.tile([P, DIM], F32)
-                nc.scalar.copy(out=result[:], in_=acc[:])
-                nc.sync.dma_start(out=out[b], in_=result[:])
-                if more:
-                    chunk_scale = softmax_scales(neg_max, part_sum)
-                row_exps = next_exps
+            for k in range(CHUNKS, TOTAL + CHUNKS + 2):
+                row_ends = k % CHUNKS == 0 and k <= TOTAL
+                if row_ends:
+                    row_top(k // CHUNKS - 1)
+                if k < TOTAL:
+                    logits(k)
+                on_scalar = k < TOTAL and k % 4 != 0
+                if k - CHUNKS < TOTAL and on_scalar:
+                    normalise(weight_stage, k - CHUNKS, True)
+                    turn(k - CHUNKS)
+                if k - 1 < TOTAL:
+                    exponentials(k - 1)
+                if row_ends:
+                    row_scales(k // CHUNKS - 1)
+                if k - CHUNKS < TOTAL and not on_scalar:
+                    normalise(weight_stage, k - CHUNKS, False)
+                    turn(k - CHUNKS)
+                if 0 <= k - CHUNKS - 1 < TOTAL:
+                    regroup(weight_stage, k - CHUNKS - 1)
+                if 0 <= k - CHUNKS - 2:
+                    quantise(weight_stage, k - CHUNKS - 2)
+                    multiply(k - CHUNKS - 2)
+                    if (k - CHUNKS - 2) % CHUNKS == CHUNKS - 1:
+                        store(weight_stage, (k - CHUNKS - 2) // CHUNKS)

@@ -22,10 +22,11 @@ PASSES = VOCAB // K_PASS
 CHUNK = 2048
 CHUNKS = VOCAB // CHUNK
 CHUNK_PASSES = CHUNK // K_PASS
+BANK_TILES = 8
 PLANES = 4
 EXP_BUFS = CHUNKS + 1
 TOTAL = BATCHES * CHUNKS
-TABLE_AHEAD = 3
+TABLE_AHEAD = 2
 TABLE_LAG = 2
 
 FLOPS = 2 * BATCHES * P * VOCAB * DIM
@@ -43,6 +44,8 @@ def tile_softembedding_k_kernel(tc, input_numeric, proj_w, proj_b, emb_table, ou
 
         identity = keep.tile([P, P], F32)
         make_identity(nc, identity[:])
+        identity_bf = keep.tile([P, P], BF16)
+        make_identity(nc, identity_bf[:])
 
         x_bf = keep.tile([P, BATCHES], BF16)
         with nc.allow_non_contiguous_dma(reason="512 scalars, one token to a partition"):
@@ -52,7 +55,14 @@ def tile_softembedding_k_kernel(tc, input_numeric, proj_w, proj_b, emb_table, ou
 
         w_all = keep.tile([P, VOCAB], BF16)
         b_all = keep.tile([P, VOCAB], BF16)
-        w_vector = proj_w.rearrange("n o -> (n o)")
+        proj_rows = keep.tile([P, 2, P], BF16)
+        nc.sync.dma_start(out=proj_rows[:, 0, :], in_=proj_w.rearrange("(t p) o -> t (p o)", p=P))
+        nc.sync.dma_start(out=proj_rows[:, 1, :], in_=proj_b.rearrange("(t p) -> t p", p=P))
+        proj_turned = psum_out.tile([P, 2, P], BF16, bufs=1)
+        nc.tensor.transpose(proj_turned[:, 0, :], proj_rows[:, 0, :], identity_bf[:])
+        nc.tensor.transpose(proj_turned[:, 1, :], proj_rows[:, 1, :], identity_bf[:])
+        proj_cols = keep.tile([P, 2, P], BF16)
+        nc.vector.tensor_copy(out=proj_cols[:], in_=proj_turned[:])
 
         table_codes = keep.tile([P, PASSES, DIM], U32, align_bytes=64)
         table_scales = keep.tile([P, PASSES // PLANES, DIM], U8, align_bytes=64)
@@ -60,10 +70,27 @@ def tile_softembedding_k_kernel(tc, input_numeric, proj_w, proj_b, emb_table, ou
         def table_plane(g):
             return table_scales[4 * (g % PLANES) : P, g // PLANES, :]
 
-        def load_projection(j):
-            cols = slice(j * CHUNK, (j + 1) * CHUNK)
-            nc.sync.dma_start(out=w_all[:, cols], in_=w_vector[cols].partition_broadcast(P))
-            nc.sync.dma_start(out=b_all[:, cols], in_=proj_b[cols].partition_broadcast(P))
+        spread_banks = {}
+
+        def spread_projection(j):
+            for which in range(2):
+                for half in range(2):
+                    bank = psum_turn.tile([P, BANK_TILES, P], BF16)
+                    for i in range(BANK_TILES):
+                        t = (2 * j + half) * BANK_TILES + i
+                        nc.tensor.transpose(
+                            bank[:, i, :], proj_cols[:, which, t : t + 1].to_broadcast([P, P]), identity_bf[:]
+                        )
+                    spread_banks[(j, which, half)] = bank
+
+        def collect_projection(j, which):
+            target = b_all if which else w_all
+            for half in range(2):
+                first = (2 * j + half) * BANK_TILES * P
+                nc.scalar.copy(
+                    out=target[:, first : first + BANK_TILES * P],
+                    in_=spread_banks[(j, which, half)][:].rearrange("p i n -> p (i n)"),
+                )
 
         table_rows = {}
         table_grouped = {}
@@ -79,10 +106,10 @@ def tile_softembedding_k_kernel(tc, input_numeric, proj_w, proj_b, emb_table, ou
             table_rows[g] = rows
 
         def regroup_table(stage, g):
-            grouped = stage.tile([P, DIM, PACK], BF16, align_bytes=64, bufs=TABLE_LAG + 1)
+            grouped = stage.tile([P, DIM, PACK], BF16, align_bytes=64, bufs=TABLE_LAG + 2)
             dst = grouped[:].rearrange("p (c i) t -> p c t i", i=4)
             src = table_rows[g][:].rearrange("p t (c i) -> p c t i", i=4)
-            if g % 3 == 0:
+            if g % 2 == 0:
                 nc.vector.tensor_copy(out=dst, in_=src)
             else:
                 nc.scalar.copy(out=dst, in_=src)
@@ -118,10 +145,13 @@ def tile_softembedding_k_kernel(tc, input_numeric, proj_w, proj_b, emb_table, ou
                 op0=ALU.mult,
                 op1=ALU.add,
             )
-            nc.vector.tensor_reduce(
-                out=neg_max[b][:, j : j + 1], in_=chunk[:], axis=AXIS.X, op=ALU.max, negate=True
-            )
             exps[k] = chunk
+
+        def maximum(k):
+            b, j = divmod(k, CHUNKS)
+            nc.vector.tensor_reduce(
+                out=neg_max[b][:, j : j + 1], in_=exps[k][:], axis=AXIS.X, op=ALU.max, negate=True
+            )
 
         def exponentials(k):
             b, j = divmod(k, CHUNKS)
@@ -232,21 +262,29 @@ def tile_softembedding_k_kernel(tc, input_numeric, proj_w, proj_b, emb_table, ou
             nc.sync.dma_start(out=out[b], in_=result[:])
 
         with tc.tile_pool(name="table_stage", bufs=1) as table_stage:
-            load_projection(0)
             for g in range(TABLE_AHEAD):
                 load_table(table_stage, g)
+            spread_projection(0)
+            collect_projection(0, 0)
+            collect_projection(0, 1)
             for k in range(CHUNKS):
                 if k + 1 < CHUNKS:
-                    load_projection(k + 1)
-                logits(k)
-                if k >= 1:
-                    exponentials(k - 1)
-                for g in range(k * CHUNK_PASSES, (k + 1) * CHUNK_PASSES):
+                    spread_projection(k + 1)
+                for quarter in range(CHUNK_PASSES):
+                    g = k * CHUNK_PASSES + quarter
                     if g + TABLE_AHEAD < PASSES:
                         load_table(table_stage, g + TABLE_AHEAD)
                     regroup_table(table_stage, g)
                     if g >= TABLE_LAG:
                         quantise_table(g - TABLE_LAG)
+                    if quarter == 0:
+                        logits(k)
+                        if k >= 1:
+                            exponentials(k - 1)
+                    if quarter == 1:
+                        maximum(k)
+                    if quarter >= 2 and k + 1 < CHUNKS:
+                        collect_projection(k + 1, quarter - 2)
             for g in range(PASSES - TABLE_LAG, PASSES):
                 quantise_table(g)
 
@@ -257,6 +295,7 @@ def tile_softembedding_k_kernel(tc, input_numeric, proj_w, proj_b, emb_table, ou
                     row_top(k // CHUNKS - 1)
                 if k < TOTAL:
                     logits(k)
+                    maximum(k)
                 on_scalar = k < TOTAL and k % 4 != 0
                 if k - CHUNKS < TOTAL and on_scalar:
                     normalise(weight_stage, k - CHUNKS, True)

@@ -35,7 +35,6 @@ FLOPS = 2 * BATCHES * P * VOCAB * DIM
 def tile_softembedding_k_kernel(tc, input_numeric, proj_w, proj_b, emb_table, out):
     nc = tc.nc
     with ExitStack() as ctx:
-        ctx.enter_context(tc.manual_schedule())
         keep = ctx.enter_context(tc.tile_pool(name="keep", bufs=1))
         exp_pool = ctx.enter_context(tc.tile_pool(name="exp_pool", bufs=EXP_BUFS))
         stats = ctx.enter_context(tc.tile_pool(name="stats", bufs=2))

@@ -23,8 +23,14 @@ CHUNK = 2048
 CHUNKS = VOCAB // CHUNK
 CHUNK_PASSES = CHUNK // K_PASS
 BANK_TILES = 8
+BANK = 512
+CHUNK_BANKS = CHUNK // BANK
+TENSOR_EVERY = 3
+TENSOR_CHUNKS = (CHUNKS + TENSOR_EVERY - 1) // TENSOR_EVERY
+VECTOR_CHUNKS = CHUNKS - TENSOR_CHUNKS
+ONES_ROW = 32
 PLANES = 4
-EXP_BUFS = CHUNKS + 1
+EXP_BUFS = CHUNKS + 2
 TOTAL = BATCHES * CHUNKS
 TABLE_AHEAD = 2
 TABLE_LAG = 2
@@ -38,8 +44,9 @@ def tile_softembedding_k_kernel(tc, input_numeric, proj_w, proj_b, emb_table, ou
         keep = ctx.enter_context(tc.tile_pool(name="keep", bufs=1))
         exp_pool = ctx.enter_context(tc.tile_pool(name="exp_pool", bufs=EXP_BUFS))
         stats = ctx.enter_context(tc.tile_pool(name="stats", bufs=2))
-        psum_turn = ctx.enter_context(tc.psum_pool(name="psum_turn", bufs=4))
-        psum_out = ctx.enter_context(tc.psum_pool(name="psum_out", bufs=2))
+        psum_logit = ctx.enter_context(tc.psum_pool(name="psum_logit", bufs=CHUNK_BANKS))
+        psum_turn = ctx.enter_context(tc.psum_pool(name="psum_turn", bufs=3))
+        psum_out = ctx.enter_context(tc.psum_pool(name="psum_out", bufs=1))
 
         identity = keep.tile([P, P], F32)
         make_identity(nc, identity[:])
@@ -52,16 +59,32 @@ def tile_softembedding_k_kernel(tc, input_numeric, proj_w, proj_b, emb_table, ou
         x_col = keep.tile([P, BATCHES], F32)
         nc.vector.tensor_copy(out=x_col[:], in_=x_bf[:])
 
-        w_all = keep.tile([P, VOCAB], BF16)
-        b_all = keep.tile([P, VOCAB], BF16)
+        w_all = keep.tile([P, VECTOR_CHUNKS * CHUNK], BF16)
+        b_all = keep.tile([P, VECTOR_CHUNKS * CHUNK], BF16)
         proj_rows = keep.tile([P, 2, P], BF16)
         nc.sync.dma_start(out=proj_rows[:, 0, :], in_=proj_w.rearrange("(t p) o -> t (p o)", p=P))
         nc.sync.dma_start(out=proj_rows[:, 1, :], in_=proj_b.rearrange("(t p) -> t p", p=P))
-        proj_turned = psum_out.tile([P, 2, P], BF16, bufs=1)
+        proj_turned = psum_out.tile([P, 2, P], BF16, tag="row_acc")
         nc.tensor.transpose(proj_turned[:, 0, :], proj_rows[:, 0, :], identity_bf[:])
         nc.tensor.transpose(proj_turned[:, 1, :], proj_rows[:, 1, :], identity_bf[:])
         proj_cols = keep.tile([P, 2, P], BF16)
         nc.vector.tensor_copy(out=proj_cols[:], in_=proj_turned[:])
+
+        x_pair = keep.tile([P, BATCHES, P], BF16)
+        nc.vector.memset(x_pair[:], 0.0)
+        nc.vector.memset(x_pair[ONES_ROW : ONES_ROW + 1, :, :], 1.0)
+        nc.sync.dma_start(out=x_pair[0:1, :, :], in_=input_numeric.rearrange("b s o -> o b s"))
+        proj_pair = keep.tile([P, TENSOR_CHUNKS, CHUNK], BF16)
+        nc.vector.memset(proj_pair[:], 0.0)
+        for i in range(TENSOR_CHUNKS):
+            cols = slice(i * TENSOR_EVERY * CHUNK, (i * TENSOR_EVERY + 1) * CHUNK)
+            nc.sync.dma_start(out=proj_pair[0:1, i, :], in_=proj_w[cols, :].rearrange("n o -> o n"))
+            nc.sync.dma_start(
+                out=proj_pair[ONES_ROW : ONES_ROW + 1, i, :], in_=proj_b[cols].unsqueeze(0)
+            )
+
+        def vector_slot(j):
+            return j - j // TENSOR_EVERY - 1
 
         table_codes = keep.tile([P, PASSES, DIM], U32, align_bytes=64)
         table_scales = keep.tile([P, PASSES // PLANES, DIM], U8, align_bytes=64)
@@ -71,21 +94,20 @@ def tile_softembedding_k_kernel(tc, input_numeric, proj_w, proj_b, emb_table, ou
 
         spread_banks = {}
 
-        def spread_projection(j):
-            for which in range(2):
-                for half in range(2):
-                    bank = psum_turn.tile([P, BANK_TILES, P], BF16)
-                    for i in range(BANK_TILES):
-                        t = (2 * j + half) * BANK_TILES + i
-                        nc.tensor.transpose(
-                            bank[:, i, :], proj_cols[:, which, t : t + 1].to_broadcast([P, P]), identity_bf[:]
-                        )
-                    spread_banks[(j, which, half)] = bank
+        def spread_projection(j, which):
+            for half in range(2):
+                bank = psum_turn.tile([P, BANK_TILES, P], BF16)
+                for i in range(BANK_TILES):
+                    t = (2 * j + half) * BANK_TILES + i
+                    nc.tensor.transpose(
+                        bank[:, i, :], proj_cols[:, which, t : t + 1].to_broadcast([P, P]), identity_bf[:]
+                    )
+                spread_banks[(j, which, half)] = bank
 
         def collect_projection(j, which):
             target = b_all if which else w_all
             for half in range(2):
-                first = (2 * j + half) * BANK_TILES * P
+                first = (2 * vector_slot(j) + half) * BANK_TILES * P
                 nc.scalar.copy(
                     out=target[:, first : first + BANK_TILES * P],
                     in_=spread_banks[(j, which, half)][:].rearrange("p i n -> p (i n)"),
@@ -122,6 +144,7 @@ def tile_softembedding_k_kernel(tc, input_numeric, proj_w, proj_b, emb_table, ou
             )
 
         exps = {}
+        logit_banks = {}
         neg_max = {}
         part_sum = {}
         neg_top = {}
@@ -131,37 +154,76 @@ def tile_softembedding_k_kernel(tc, input_numeric, proj_w, proj_b, emb_table, ou
             b, j = divmod(k, CHUNKS)
             if j == 0:
                 row_neg_max = stats.tile([P, CHUNKS], F32)
-                row_part_sum = stats.tile([P, CHUNKS], F32)
+                row_part_sum = stats.tile([P, CHUNKS, CHUNK_BANKS], F32)
+                nc.vector.memset(row_part_sum[:], 0.0)
                 neg_max[b] = row_neg_max
                 part_sum[b] = row_part_sum
-            cols = slice(j * CHUNK, (j + 1) * CHUNK)
             chunk = exp_pool.tile([P, CHUNK], F32)
-            nc.vector.scalar_tensor_tensor(
-                out=chunk[:],
-                in0=w_all[:, cols],
-                scalar=x_col[:, b : b + 1],
-                in1=b_all[:, cols],
-                op0=ALU.mult,
-                op1=ALU.add,
-            )
             exps[k] = chunk
+            if j % TENSOR_EVERY == 0:
+                logit_banks[k] = []
+                for q in range(CHUNK_BANKS):
+                    logit_bank = psum_logit.tile([P, BANK], F32)
+                    nc.tensor.matmul(
+                        out=logit_bank[:],
+                        lhsT=x_pair[:, b, :],
+                        rhs=proj_pair[:, j // TENSOR_EVERY, q * BANK : (q + 1) * BANK],
+                        start=True,
+                        stop=True,
+                    )
+                    logit_banks[k].append(logit_bank)
+            else:
+                cols = slice(vector_slot(j) * CHUNK, (vector_slot(j) + 1) * CHUNK)
+                nc.vector.scalar_tensor_tensor(
+                    out=chunk[:],
+                    in0=w_all[:, cols],
+                    scalar=x_col[:, b : b + 1],
+                    in1=b_all[:, cols],
+                    op0=ALU.mult,
+                    op1=ALU.add,
+                )
 
         def maximum(k):
             b, j = divmod(k, CHUNKS)
-            nc.vector.tensor_reduce(
-                out=neg_max[b][:, j : j + 1], in_=exps[k][:], axis=AXIS.X, op=ALU.max, negate=True
-            )
+            if j % TENSOR_EVERY == 0:
+                bank_neg_max = stats.tile([P, CHUNK_BANKS], F32)
+                for q in range(CHUNK_BANKS):
+                    nc.vector.tensor_reduce(
+                        out=bank_neg_max[:, q : q + 1],
+                        in_=logit_banks[k][q][:],
+                        axis=AXIS.X,
+                        op=ALU.max,
+                        negate=True,
+                    )
+                nc.vector.tensor_reduce(
+                    out=neg_max[b][:, j : j + 1], in_=bank_neg_max[:], axis=AXIS.X, op=ALU.min
+                )
+            else:
+                nc.vector.tensor_reduce(
+                    out=neg_max[b][:, j : j + 1], in_=exps[k][:], axis=AXIS.X, op=ALU.max, negate=True
+                )
 
         def exponentials(k):
             b, j = divmod(k, CHUNKS)
-            nc.scalar.activation(
-                out=exps[k][:],
-                in_=exps[k][:],
-                func=ACT.Exp,
-                bias=neg_max[b][:, j : j + 1],
-                scale=1.0,
-                accum_out=part_sum[b][:, j : j + 1],
-            )
+            if j % TENSOR_EVERY == 0:
+                for q in range(CHUNK_BANKS):
+                    nc.scalar.activation(
+                        out=exps[k][:, q * BANK : (q + 1) * BANK],
+                        in_=logit_banks[k][q][:],
+                        func=ACT.Exp,
+                        bias=neg_max[b][:, j : j + 1],
+                        scale=1.0,
+                        accum_out=part_sum[b][:, j, q : q + 1],
+                    )
+            else:
+                nc.scalar.activation(
+                    out=exps[k][:],
+                    in_=exps[k][:],
+                    func=ACT.Exp,
+                    bias=neg_max[b][:, j : j + 1],
+                    scale=1.0,
+                    accum_out=part_sum[b][:, j, 0:1],
+                )
 
         def row_top(b):
             top = stats.tile([P, 1], F32)
@@ -173,8 +235,10 @@ def tile_softembedding_k_kernel(tc, input_numeric, proj_w, proj_b, emb_table, ou
             nc.scalar.activation(
                 out=factor[:], in_=neg_max[b][:], func=ACT.Exp, bias=neg_top[b][:, 0:1], scale=-1.0
             )
+            chunk_sum = stats.tile([P, CHUNKS], F32)
+            nc.vector.tensor_reduce(out=chunk_sum[:], in_=part_sum[b][:], axis=AXIS.X, op=ALU.add)
             weighted = stats.tile([P, CHUNKS], F32)
-            nc.vector.tensor_tensor(out=weighted[:], in0=factor[:], in1=part_sum[b][:], op=ALU.mult)
+            nc.vector.tensor_tensor(out=weighted[:], in0=factor[:], in1=chunk_sum[:], op=ALU.mult)
             total = stats.tile([P, 1], F32)
             nc.vector.tensor_reduce(out=total[:], in_=weighted[:], axis=AXIS.X, op=ALU.add)
             inv_total = stats.tile([P, 1], F32)
@@ -263,12 +327,8 @@ def tile_softembedding_k_kernel(tc, input_numeric, proj_w, proj_b, emb_table, ou
         with tc.tile_pool(name="table_stage", bufs=1) as table_stage:
             for g in range(TABLE_AHEAD):
                 load_table(table_stage, g)
-            spread_projection(0)
-            collect_projection(0, 0)
-            collect_projection(0, 1)
             for k in range(CHUNKS):
-                if k + 1 < CHUNKS:
-                    spread_projection(k + 1)
+                spread_next = k + 1 < CHUNKS and (k + 1) % TENSOR_EVERY != 0
                 for quarter in range(CHUNK_PASSES):
                     g = k * CHUNK_PASSES + quarter
                     if g + TABLE_AHEAD < PASSES:
@@ -282,7 +342,9 @@ def tile_softembedding_k_kernel(tc, input_numeric, proj_w, proj_b, emb_table, ou
                             exponentials(k - 1)
                     if quarter == 1:
                         maximum(k)
-                    if quarter >= 2 and k + 1 < CHUNKS:
+                    if quarter < 2 and spread_next:
+                        spread_projection(k + 1, quarter)
+                    if quarter >= 2 and spread_next:
                         collect_projection(k + 1, quarter - 2)
             for g in range(PASSES - TABLE_LAG, PASSES):
                 quantise_table(g)
@@ -295,7 +357,7 @@ def tile_softembedding_k_kernel(tc, input_numeric, proj_w, proj_b, emb_table, ou
                 if k < TOTAL:
                     logits(k)
                     maximum(k)
-                on_scalar = k < TOTAL and k % 4 != 0
+                on_scalar = k < TOTAL and k % 2 == 1
                 if k - CHUNKS < TOTAL and on_scalar:
                     normalise(weight_stage, k - CHUNKS, True)
                     turn(k - CHUNKS)

@@ -357,7 +357,7 @@ def tile_softembedding_k_kernel(tc, input_numeric, proj_w, proj_b, emb_table, ou
                 if k < TOTAL:
                     logits(k)
                     maximum(k)
-                on_scalar = k < TOTAL and k % 2 == 1
+                on_scalar = k < TOTAL and k % 3 != 0 and not row_ends
                 if k - CHUNKS < TOTAL and on_scalar:
                     normalise(weight_stage, k - CHUNKS, True)
                     turn(k - CHUNKS)

@@ -22,18 +22,25 @@ PASSES = VOCAB // K_PASS
 CHUNK = 2048
 CHUNKS = VOCAB // CHUNK
 CHUNK_PASSES = CHUNK // K_PASS
-BANK_TILES = 8
+TOTAL = BATCHES * CHUNKS
 BANK = 512
 CHUNK_BANKS = CHUNK // BANK
+BANK_TILES = 8
+SPREAD_BANKS = CHUNK // (BANK_TILES * P)
+BANK_PASSES = 2
+PLANES = 4
+PLANE_ROWS = 4
+RUN = 4
 TENSOR_EVERY = 3
 TENSOR_CHUNKS = (CHUNKS + TENSOR_EVERY - 1) // TENSOR_EVERY
 VECTOR_CHUNKS = CHUNKS - TENSOR_CHUNKS
-ONES_ROW = 32
-PLANES = 4
+ONES_PARTITION = 32
 EXP_BUFS = CHUNKS + 2
-TOTAL = BATCHES * CHUNKS
 TABLE_AHEAD = 2
 TABLE_LAG = 2
+NORMALISE_LAG = CHUNKS
+REGROUP_LAG = NORMALISE_LAG + 1
+MULTIPLY_LAG = NORMALISE_LAG + 2
 
 FLOPS = 2 * BATCHES * P * VOCAB * DIM
 
@@ -61,18 +68,18 @@ def tile_softembedding_k_kernel(tc, input_numeric, proj_w, proj_b, emb_table, ou
 
         w_all = keep.tile([P, VECTOR_CHUNKS * CHUNK], BF16)
         b_all = keep.tile([P, VECTOR_CHUNKS * CHUNK], BF16)
-        proj_rows = keep.tile([P, 2, P], BF16)
-        nc.sync.dma_start(out=proj_rows[:, 0, :], in_=proj_w.rearrange("(t p) o -> t (p o)", p=P))
-        nc.sync.dma_start(out=proj_rows[:, 1, :], in_=proj_b.rearrange("(t p) -> t p", p=P))
+        proj_loaded = keep.tile([P, 2, P], BF16)
+        nc.sync.dma_start(out=proj_loaded[:, 0, :], in_=proj_w.rearrange("(a p) o -> a (p o)", p=P))
+        nc.sync.dma_start(out=proj_loaded[:, 1, :], in_=proj_b.rearrange("(a p) -> a p", p=P))
         proj_turned = psum_out.tile([P, 2, P], BF16, tag="row_acc")
-        nc.tensor.transpose(proj_turned[:, 0, :], proj_rows[:, 0, :], identity_bf[:])
-        nc.tensor.transpose(proj_turned[:, 1, :], proj_rows[:, 1, :], identity_bf[:])
+        nc.tensor.transpose(proj_turned[:, 0, :], proj_loaded[:, 0, :], identity_bf[:])
+        nc.tensor.transpose(proj_turned[:, 1, :], proj_loaded[:, 1, :], identity_bf[:])
         proj_cols = keep.tile([P, 2, P], BF16)
         nc.vector.tensor_copy(out=proj_cols[:], in_=proj_turned[:])
 
         x_pair = keep.tile([P, BATCHES, P], BF16)
         nc.vector.memset(x_pair[:], 0.0)
-        nc.vector.memset(x_pair[ONES_ROW : ONES_ROW + 1, :, :], 1.0)
+        nc.vector.memset(x_pair[ONES_PARTITION : ONES_PARTITION + 1, :, :], 1.0)
         nc.sync.dma_start(out=x_pair[0:1, :, :], in_=input_numeric.rearrange("b s o -> o b s"))
         proj_pair = keep.tile([P, TENSOR_CHUNKS, CHUNK], BF16)
         nc.vector.memset(proj_pair[:], 0.0)
@@ -80,7 +87,7 @@ def tile_softembedding_k_kernel(tc, input_numeric, proj_w, proj_b, emb_table, ou
             cols = slice(i * TENSOR_EVERY * CHUNK, (i * TENSOR_EVERY + 1) * CHUNK)
             nc.sync.dma_start(out=proj_pair[0:1, i, :], in_=proj_w[cols, :].rearrange("n o -> o n"))
             nc.sync.dma_start(
-                out=proj_pair[ONES_ROW : ONES_ROW + 1, i, :], in_=proj_b[cols].unsqueeze(0)
+                out=proj_pair[ONES_PARTITION : ONES_PARTITION + 1, i, :], in_=proj_b[cols].unsqueeze(0)
             )
 
         def vector_slot(j):
@@ -90,24 +97,26 @@ def tile_softembedding_k_kernel(tc, input_numeric, proj_w, proj_b, emb_table, ou
         table_scales = keep.tile([P, PASSES // PLANES, DIM], U8, align_bytes=64)
 
         def table_plane(g):
-            return table_scales[4 * (g % PLANES) : P, g // PLANES, :]
+            return table_scales[PLANE_ROWS * (g % PLANES) : P, g // PLANES, :]
 
         spread_banks = {}
 
         def spread_projection(j, which):
-            for half in range(2):
-                bank = psum_turn.tile([P, BANK_TILES, P], BF16)
+            for half in range(SPREAD_BANKS):
+                spread_bank = psum_turn.tile([P, BANK_TILES, P], BF16, tag="turn_bank")
                 for i in range(BANK_TILES):
-                    t = (2 * j + half) * BANK_TILES + i
+                    a = (SPREAD_BANKS * j + half) * BANK_TILES + i
                     nc.tensor.transpose(
-                        bank[:, i, :], proj_cols[:, which, t : t + 1].to_broadcast([P, P]), identity_bf[:]
+                        spread_bank[:, i, :],
+                        proj_cols[:, which, a : a + 1].to_broadcast([P, P]),
+                        identity_bf[:],
                     )
-                spread_banks[(j, which, half)] = bank
+                spread_banks[(j, which, half)] = spread_bank
 
         def collect_projection(j, which):
             target = b_all if which else w_all
-            for half in range(2):
-                first = (2 * vector_slot(j) + half) * BANK_TILES * P
+            for half in range(SPREAD_BANKS):
+                first = (SPREAD_BANKS * vector_slot(j) + half) * BANK_TILES * P
                 nc.scalar.copy(
                     out=target[:, first : first + BANK_TILES * P],
                     in_=spread_banks[(j, which, half)][:].rearrange("p i n -> p (i n)"),
@@ -117,24 +126,24 @@ def tile_softembedding_k_kernel(tc, input_numeric, proj_w, proj_b, emb_table, ou
         table_grouped = {}
 
         def load_table(stage, g):
-            rows = stage.tile([P, PACK, DIM], BF16, bufs=TABLE_AHEAD + 1)
+            pass_rows = stage.tile([P, PACK, DIM], BF16, bufs=TABLE_AHEAD + 1)
             nc.sync.dma_start(
-                out=rows[:].rearrange("p (u e) d -> p u (e d)", u=2),
+                out=pass_rows[:].rearrange("p (u e) d -> p u (e d)", u=2),
                 in_=emb_table[g * K_PASS : (g + 1) * K_PASS, :].rearrange(
                     "(u p e) d -> p u (e d)", u=2, e=2
                 ),
             )
-            table_rows[g] = rows
+            table_rows[g] = pass_rows
 
         def regroup_table(stage, g):
-            grouped = stage.tile([P, DIM, PACK], BF16, align_bytes=64, bufs=TABLE_LAG + 2)
-            dst = grouped[:].rearrange("p (c i) t -> p c t i", i=4)
-            src = table_rows[g][:].rearrange("p t (c i) -> p c t i", i=4)
+            pass_grouped = stage.tile([P, DIM, PACK], BF16, align_bytes=64, bufs=TABLE_LAG + 2)
+            dst = pass_grouped[:].rearrange("p (r i) t -> p r t i", i=RUN)
+            src = table_rows[g][:].rearrange("p t (r i) -> p r t i", i=RUN)
             if g % 2 == 0:
                 nc.vector.tensor_copy(out=dst, in_=src)
             else:
                 nc.scalar.copy(out=dst, in_=src)
-            table_grouped[g] = grouped
+            table_grouped[g] = pass_grouped
 
         def quantise_table(g):
             nc.vector.quantize_mx(
@@ -162,12 +171,12 @@ def tile_softembedding_k_kernel(tc, input_numeric, proj_w, proj_b, emb_table, ou
             exps[k] = chunk
             if j % TENSOR_EVERY == 0:
                 logit_banks[k] = []
-                for q in range(CHUNK_BANKS):
+                for bank_no in range(CHUNK_BANKS):
                     logit_bank = psum_logit.tile([P, BANK], F32)
                     nc.tensor.matmul(
                         out=logit_bank[:],
                         lhsT=x_pair[:, b, :],
-                        rhs=proj_pair[:, j // TENSOR_EVERY, q * BANK : (q + 1) * BANK],
+                        rhs=proj_pair[:, j // TENSOR_EVERY, bank_no * BANK : (bank_no + 1) * BANK],
                         start=True,
                         stop=True,
                     )
@@ -187,10 +196,10 @@ def tile_softembedding_k_kernel(tc, input_numeric, proj_w, proj_b, emb_table, ou
             b, j = divmod(k, CHUNKS)
             if j % TENSOR_EVERY == 0:
                 bank_neg_max = stats.tile([P, CHUNK_BANKS], F32)
-                for q in range(CHUNK_BANKS):
+                for bank_no in range(CHUNK_BANKS):
                     nc.vector.tensor_reduce(
-                        out=bank_neg_max[:, q : q + 1],
-                        in_=logit_banks[k][q][:],
+                        out=bank_neg_max[:, bank_no : bank_no + 1],
+                        in_=logit_banks[k][bank_no][:],
                         axis=AXIS.X,
                         op=ALU.max,
                         negate=True,
@@ -206,14 +215,14 @@ def tile_softembedding_k_kernel(tc, input_numeric, proj_w, proj_b, emb_table, ou
         def exponentials(k):
             b, j = divmod(k, CHUNKS)
             if j % TENSOR_EVERY == 0:
-                for q in range(CHUNK_BANKS):
+                for bank_no in range(CHUNK_BANKS):
                     nc.scalar.activation(
-                        out=exps[k][:, q * BANK : (q + 1) * BANK],
-                        in_=logit_banks[k][q][:],
+                        out=exps[k][:, bank_no * BANK : (bank_no + 1) * BANK],
+                        in_=logit_banks[k][bank_no][:],
                         func=ACT.Exp,
                         bias=neg_max[b][:, j : j + 1],
                         scale=1.0,
-                        accum_out=part_sum[b][:, j, q : q + 1],
+                        accum_out=part_sum[b][:, j, bank_no : bank_no + 1],
                     )
             else:
                 nc.scalar.activation(
@@ -243,13 +252,13 @@ def tile_softembedding_k_kernel(tc, input_numeric, proj_w, proj_b, emb_table, ou
             nc.vector.tensor_reduce(out=total[:], in_=weighted[:], axis=AXIS.X, op=ALU.add)
             inv_total = stats.tile([P, 1], F32)
             nc.vector.reciprocal(out=inv_total[:], in_=total[:])
-            scales = stats.tile([P, CHUNKS], F32)
+            row_chunk_scale = stats.tile([P, CHUNKS], F32)
             nc.vector.tensor_scalar(
-                out=scales[:], in0=factor[:], scalar1=inv_total[:, 0:1], scalar2=None, op0=ALU.mult
+                out=row_chunk_scale[:], in0=factor[:], scalar1=inv_total[:, 0:1], scalar2=None, op0=ALU.mult
             )
-            chunk_scale[b] = scales
+            chunk_scale[b] = row_chunk_scale
 
-        weight_rows = {}
+        weights = {}
         turned = {}
         weight_grouped = {}
         weight_codes = {}
@@ -258,48 +267,54 @@ def tile_softembedding_k_kernel(tc, input_numeric, proj_w, proj_b, emb_table, ou
 
         def normalise(stage, k, on_scalar):
             b, j = divmod(k, CHUNKS)
-            rows = stage.tile([P, CHUNK], BF16)
+            chunk_weights = stage.tile([P, CHUNK], BF16)
             if on_scalar:
                 nc.scalar.activation(
-                    out=rows[:], in_=exps[k][:], func=ACT.Copy, scale=chunk_scale[b][:, j : j + 1]
+                    out=chunk_weights[:], in_=exps[k][:], func=ACT.Copy, scale=chunk_scale[b][:, j : j + 1]
                 )
             else:
                 nc.vector.tensor_scalar(
-                    out=rows[:], in0=exps[k][:], scalar1=chunk_scale[b][:, j : j + 1], scalar2=None, op0=ALU.mult
+                    out=chunk_weights[:],
+                    in0=exps[k][:],
+                    scalar1=chunk_scale[b][:, j : j + 1],
+                    scalar2=None,
+                    op0=ALU.mult,
                 )
-            weight_rows[k] = rows
+            weights[k] = chunk_weights
 
         def turn(k):
-            words = weight_rows[k][:].bitcast(F32)
+            words = weights[k][:].bitcast(F32)
             turned[k] = []
-            for half in range(CHUNK_PASSES // 2):
-                bank = psum_turn.tile([P, 2, 2, P], F32)
-                for c in range(2):
+            for half in range(CHUNK_PASSES // BANK_PASSES):
+                turned_bank = psum_turn.tile([P, BANK_PASSES, 2, P], F32, tag="turn_bank")
+                for c in range(BANK_PASSES):
                     for u in range(2):
-                        first = ((2 * half + c) * 2 + u) * P
-                        nc.tensor.transpose(bank[:, c, u, :], words[:, first : first + P], identity[:])
-                turned[k].append(bank)
+                        first = ((BANK_PASSES * half + c) * 2 + u) * P
+                        nc.tensor.transpose(
+                            turned_bank[:, c, u, :], words[:, first : first + P], identity[:]
+                        )
+                turned[k].append(turned_bank)
 
         def regroup(stage, k):
-            grouped = stage.tile([P, CHUNK_PASSES, P, PACK], BF16, align_bytes=64)
-            grouped_words = grouped[:].bitcast(F32)
-            for half in range(CHUNK_PASSES // 2):
+            chunk_grouped = stage.tile([P, CHUNK_PASSES, P, PACK], BF16, align_bytes=64)
+            grouped_words = chunk_grouped[:].bitcast(F32)
+            for half in range(CHUNK_PASSES // BANK_PASSES):
                 nc.scalar.copy(
-                    out=grouped_words[:, 2 * half : 2 * half + 2, :, :],
-                    in_=turned[k][half][:].rearrange("p c u m -> p c m u"),
+                    out=grouped_words[:, BANK_PASSES * half : BANK_PASSES * (half + 1), :, :],
+                    in_=turned[k][half][:].rearrange("p c u s -> p c s u"),
                 )
-            weight_grouped[k] = grouped
+            weight_grouped[k] = chunk_grouped
 
         def quantise(stage, k):
-            codes = stage.tile([P, CHUNK_PASSES * P], U32, align_bytes=64)
-            scales = stage.tile([P, CHUNK_PASSES * P], U8, align_bytes=64)
+            chunk_codes = stage.tile([P, CHUNK_PASSES * P], U32, align_bytes=64)
+            chunk_planes = stage.tile([P, CHUNK_PASSES * P], U8, align_bytes=64)
             nc.vector.quantize_mx(
-                out=codes[:].bitcast(FP8X4),
-                scales=scales[:],
-                in_=weight_grouped[k][:].rearrange("p c m t -> p (c m t)"),
+                out=chunk_codes[:].bitcast(FP8X4),
+                scales=chunk_planes[:],
+                in_=weight_grouped[k][:].rearrange("p c s t -> p (c s t)"),
             )
-            weight_codes[k] = codes
-            weight_scales[k] = scales
+            weight_codes[k] = chunk_codes
+            weight_scales[k] = chunk_planes
 
         def multiply(k):
             b, j = divmod(k, CHUNKS)
@@ -323,6 +338,7 @@ def tile_softembedding_k_kernel(tc, input_numeric, proj_w, proj_b, emb_table, ou
             result = stage.tile([P, DIM], F32)
             nc.scalar.copy(out=result[:], in_=acc[b][:])
             nc.sync.dma_start(out=out[b], in_=result[:])
+
 
         with tc.tile_pool(name="table_stage", bufs=1) as table_stage:
             for g in range(TABLE_AHEAD):
@@ -350,28 +366,28 @@ def tile_softembedding_k_kernel(tc, input_numeric, proj_w, proj_b, emb_table, ou
                 quantise_table(g)
 
         with tc.tile_pool(name="weight_stage", bufs=2, reuse_waits="tile") as weight_stage:
-            for k in range(CHUNKS, TOTAL + CHUNKS + 2):
+            for k in range(CHUNKS, TOTAL + MULTIPLY_LAG):
                 row_ends = k % CHUNKS == 0 and k <= TOTAL
                 if row_ends:
                     row_top(k // CHUNKS - 1)
                 if k < TOTAL:
                     logits(k)
                     maximum(k)
-                on_scalar = k < TOTAL and k % 3 != 0 and not row_ends
-                if k - CHUNKS < TOTAL and on_scalar:
-                    normalise(weight_stage, k - CHUNKS, True)
-                    turn(k - CHUNKS)
+                on_scalar = k < TOTAL and k % 2 == 1
+                if k - NORMALISE_LAG < TOTAL and on_scalar:
+                    normalise(weight_stage, k - NORMALISE_LAG, True)
+                    turn(k - NORMALISE_LAG)
                 if k - 1 < TOTAL:
                     exponentials(k - 1)
                 if row_ends:
                     row_scales(k // CHUNKS - 1)
-                if k - CHUNKS < TOTAL and not on_scalar:
-                    normalise(weight_stage, k - CHUNKS, False)
-                    turn(k - CHUNKS)
-                if 0 <= k - CHUNKS - 1 < TOTAL:
-                    regroup(weight_stage, k - CHUNKS - 1)
-                if 0 <= k - CHUNKS - 2:
-                    quantise(weight_stage, k - CHUNKS - 2)
-                    multiply(k - CHUNKS - 2)
-                    if (k - CHUNKS - 2) % CHUNKS == CHUNKS - 1:
-                        store(weight_stage, (k - CHUNKS - 2) // CHUNKS)
+                if k - NORMALISE_LAG < TOTAL and not on_scalar:
+                    normalise(weight_stage, k - NORMALISE_LAG, False)
+                    turn(k - NORMALISE_LAG)
+                if 0 <= k - REGROUP_LAG < TOTAL:
+                    regroup(weight_stage, k - REGROUP_LAG)
+                if 0 <= k - MULTIPLY_LAG:
+                    quantise(weight_stage, k - MULTIPLY_LAG)
+                    multiply(k - MULTIPLY_LAG)
+                    if (k - MULTIPLY_LAG) % CHUNKS == CHUNKS - 1:
+                        store(weight_stage, (k - MULTIPLY_LAG) // CHUNKS)

from contextlib import ExitStack

import concourse.mybir as mybir
from concourse.masks import make_identity

F32 = mybir.dt.float32
BF16 = mybir.dt.bfloat16
U32 = mybir.dt.uint32
U8 = mybir.dt.uint8
FP8X4 = mybir.dt.float8_e4m3fn_x4
ALU = mybir.AluOpType
ACT = mybir.ActivationFunctionType
AXIS = mybir.AxisListType

P = 128
BATCHES = 4
VOCAB = 16384
DIM = 512
PACK = 4
K_PASS = P * PACK
PASSES = VOCAB // K_PASS
CHUNK = 2048
CHUNKS = VOCAB // CHUNK
CHUNK_PASSES = CHUNK // K_PASS
TOTAL = BATCHES * CHUNKS
BANK = 512
CHUNK_BANKS = CHUNK // BANK
BANK_TILES = 8
SPREAD_BANKS = CHUNK // (BANK_TILES * P)
BANK_PASSES = 2
PLANES = 4
PLANE_ROWS = 4
RUN = 4
TENSOR_EVERY = 3
TENSOR_CHUNKS = (CHUNKS + TENSOR_EVERY - 1) // TENSOR_EVERY
VECTOR_CHUNKS = CHUNKS - TENSOR_CHUNKS
ONES_PARTITION = 32
EXP_BUFS = CHUNKS + 2
TABLE_AHEAD = 2
TABLE_LAG = 2
NORMALISE_LAG = CHUNKS
REGROUP_LAG = NORMALISE_LAG + 1
MULTIPLY_LAG = NORMALISE_LAG + 2

FLOPS = 2 * BATCHES * P * VOCAB * DIM


def tile_softembedding_k_kernel(tc, input_numeric, proj_w, proj_b, emb_table, out):
    nc = tc.nc
    with ExitStack() as ctx:
        keep = ctx.enter_context(tc.tile_pool(name="keep", bufs=1))
        exp_pool = ctx.enter_context(tc.tile_pool(name="exp_pool", bufs=EXP_BUFS))
        stats = ctx.enter_context(tc.tile_pool(name="stats", bufs=2))
        psum_logit = ctx.enter_context(tc.psum_pool(name="psum_logit", bufs=CHUNK_BANKS))
        psum_turn = ctx.enter_context(tc.psum_pool(name="psum_turn", bufs=3))
        psum_out = ctx.enter_context(tc.psum_pool(name="psum_out", bufs=1))

        identity = keep.tile([P, P], F32)
        make_identity(nc, identity[:])
        identity_bf = keep.tile([P, P], BF16)
        make_identity(nc, identity_bf[:])

        x_bf = keep.tile([P, BATCHES], BF16)
        with nc.allow_non_contiguous_dma(reason="512 scalars, one token to a partition"):
            nc.sync.dma_start(out=x_bf[:], in_=input_numeric.rearrange("b s o -> s (b o)"))
        x_col = keep.tile([P, BATCHES], F32)
        nc.vector.tensor_copy(out=x_col[:], in_=x_bf[:])

        w_all = keep.tile([P, VECTOR_CHUNKS * CHUNK], BF16)
        b_all = keep.tile([P, VECTOR_CHUNKS * CHUNK], BF16)
        proj_loaded = keep.tile([P, 2, P], BF16)
        nc.sync.dma_start(out=proj_loaded[:, 0, :], in_=proj_w.rearrange("(a p) o -> a (p o)", p=P))
        nc.sync.dma_start(out=proj_loaded[:, 1, :], in_=proj_b.rearrange("(a p) -> a p", p=P))
        proj_turned = psum_out.tile([P, 2, P], BF16, tag="row_acc")
        nc.tensor.transpose(proj_turned[:, 0, :], proj_loaded[:, 0, :], identity_bf[:])
        nc.tensor.transpose(proj_turned[:, 1, :], proj_loaded[:, 1, :], identity_bf[:])
        proj_cols = keep.tile([P, 2, P], BF16)
        nc.vector.tensor_copy(out=proj_cols[:], in_=proj_turned[:])

        x_pair = keep.tile([P, BATCHES, P], BF16)
        nc.vector.memset(x_pair[:], 0.0)
        nc.vector.memset(x_pair[ONES_PARTITION : ONES_PARTITION + 1, :, :], 1.0)
        nc.sync.dma_start(out=x_pair[0:1, :, :], in_=input_numeric.rearrange("b s o -> o b s"))
        proj_pair = keep.tile([P, TENSOR_CHUNKS, CHUNK], BF16)
        nc.vector.memset(proj_pair[:], 0.0)
        for i in range(TENSOR_CHUNKS):
            cols = slice(i * TENSOR_EVERY * CHUNK, (i * TENSOR_EVERY + 1) * CHUNK)
            nc.sync.dma_start(out=proj_pair[0:1, i, :], in_=proj_w[cols, :].rearrange("n o -> o n"))
            nc.sync.dma_start(
                out=proj_pair[ONES_PARTITION : ONES_PARTITION + 1, i, :], in_=proj_b[cols].unsqueeze(0)
            )

        def vector_slot(j):
            return j - j // TENSOR_EVERY - 1

        table_codes = keep.tile([P, PASSES, DIM], U32, align_bytes=64)
        table_scales = keep.tile([P, PASSES // PLANES, DIM], U8, align_bytes=64)

        def table_plane(g):
            return table_scales[PLANE_ROWS * (g % PLANES) : P, g // PLANES, :]

        spread_banks = {}

        def spread_projection(j, which):
            for half in range(SPREAD_BANKS):
                spread_bank = psum_turn.tile([P, BANK_TILES, P], BF16, tag="turn_bank")
                for i in range(BANK_TILES):
                    a = (SPREAD_BANKS * j + half) * BANK_TILES + i
                    nc.tensor.transpose(
                        spread_bank[:, i, :],
                        proj_cols[:, which, a : a + 1].to_broadcast([P, P]),
                        identity_bf[:],
                    )
                spread_banks[(j, which, half)] = spread_bank

        def collect_projection(j, which):
            target = b_all if which else w_all
            for half in range(SPREAD_BANKS):
                first = (SPREAD_BANKS * vector_slot(j) + half) * BANK_TILES * P
                nc.scalar.copy(
                    out=target[:, first : first + BANK_TILES * P],
                    in_=spread_banks[(j, which, half)][:].rearrange("p i n -> p (i n)"),
                )

        table_rows = {}
        table_grouped = {}

        def load_table(stage, g):
            pass_rows = stage.tile([P, PACK, DIM], BF16, bufs=TABLE_AHEAD + 1)
            nc.sync.dma_start(
                out=pass_rows[:].rearrange("p (u e) d -> p u (e d)", u=2),
                in_=emb_table[g * K_PASS : (g + 1) * K_PASS, :].rearrange(
                    "(u p e) d -> p u (e d)", u=2, e=2
                ),
            )
            table_rows[g] = pass_rows

        def regroup_table(stage, g):
            pass_grouped = stage.tile([P, DIM, PACK], BF16, align_bytes=64, bufs=TABLE_LAG + 2)
            dst = pass_grouped[:].rearrange("p (r i) t -> p r t i", i=RUN)
            src = table_rows[g][:].rearrange("p t (r i) -> p r t i", i=RUN)
            if g % 2 == 0:
                nc.vector.tensor_copy(out=dst, in_=src)
            else:
                nc.scalar.copy(out=dst, in_=src)
            table_grouped[g] = pass_grouped

        def quantise_table(g):
            nc.vector.quantize_mx(
                out=table_codes[:, g, :].bitcast(FP8X4),
                scales=table_plane(g),
                in_=table_grouped[g][:].rearrange("p d t -> p (d t)"),
            )

        exps = {}
        logit_banks = {}
        neg_max = {}
        part_sum = {}
        neg_top = {}
        chunk_scale = {}

        def logits(k):
            b, j = divmod(k, CHUNKS)
            if j == 0:
                row_neg_max = stats.tile([P, CHUNKS], F32)
                row_part_sum = stats.tile([P, CHUNKS, CHUNK_BANKS], F32)
                nc.vector.memset(row_part_sum[:], 0.0)
                neg_max[b] = row_neg_max
                part_sum[b] = row_part_sum
            chunk = exp_pool.tile([P, CHUNK], F32)
            exps[k] = chunk
            if j % TENSOR_EVERY == 0:
                logit_banks[k] = []
                for bank_no in range(CHUNK_BANKS):
                    logit_bank = psum_logit.tile([P, BANK], F32)
                    nc.tensor.matmul(
                        out=logit_bank[:],
                        lhsT=x_pair[:, b, :],
                        rhs=proj_pair[:, j // TENSOR_EVERY, bank_no * BANK : (bank_no + 1) * BANK],
                        start=True,
                        stop=True,
                    )
                    logit_banks[k].append(logit_bank)
            else:
                cols = slice(vector_slot(j) * CHUNK, (vector_slot(j) + 1) * CHUNK)
                nc.vector.scalar_tensor_tensor(
                    out=chunk[:],
                    in0=w_all[:, cols],
                    scalar=x_col[:, b : b + 1],
                    in1=b_all[:, cols],
                    op0=ALU.mult,
                    op1=ALU.add,
                )

        def maximum(k):
            b, j = divmod(k, CHUNKS)
            if j % TENSOR_EVERY == 0:
                bank_neg_max = stats.tile([P, CHUNK_BANKS], F32)
                for bank_no in range(CHUNK_BANKS):
                    nc.vector.tensor_reduce(
                        out=bank_neg_max[:, bank_no : bank_no + 1],
                        in_=logit_banks[k][bank_no][:],
                        axis=AXIS.X,
                        op=ALU.max,
                        negate=True,
                    )
                nc.vector.tensor_reduce(
                    out=neg_max[b][:, j : j + 1], in_=bank_neg_max[:], axis=AXIS.X, op=ALU.min
                )
            else:
                nc.vector.tensor_reduce(
                    out=neg_max[b][:, j : j + 1], in_=exps[k][:], axis=AXIS.X, op=ALU.max, negate=True
                )

        def exponentials(k):
            b, j = divmod(k, CHUNKS)
            if j % TENSOR_EVERY == 0:
                for bank_no in range(CHUNK_BANKS):
                    nc.scalar.activation(
                        out=exps[k][:, bank_no * BANK : (bank_no + 1) * BANK],
                        in_=logit_banks[k][bank_no][:],
                        func=ACT.Exp,
                        bias=neg_max[b][:, j : j + 1],
                        scale=1.0,
                        accum_out=part_sum[b][:, j, bank_no : bank_no + 1],
                    )
            else:
                nc.scalar.activation(
                    out=exps[k][:],
                    in_=exps[k][:],
                    func=ACT.Exp,
                    bias=neg_max[b][:, j : j + 1],
                    scale=1.0,
                    accum_out=part_sum[b][:, j, 0:1],
                )

        def row_top(b):
            top = stats.tile([P, 1], F32)
            nc.vector.tensor_reduce(out=top[:], in_=neg_max[b][:], axis=AXIS.X, op=ALU.min)
            neg_top[b] = top

        def row_scales(b):
            factor = stats.tile([P, CHUNKS], F32)
            nc.scalar.activation(
                out=factor[:], in_=neg_max[b][:], func=ACT.Exp, bias=neg_top[b][:, 0:1], scale=-1.0
            )
            chunk_sum = stats.tile([P, CHUNKS], F32)
            nc.vector.tensor_reduce(out=chunk_sum[:], in_=part_sum[b][:], axis=AXIS.X, op=ALU.add)
            weighted = stats.tile([P, CHUNKS], F32)
            nc.vector.tensor_tensor(out=weighted[:], in0=factor[:], in1=chunk_sum[:], op=ALU.mult)
            total = stats.tile([P, 1], F32)
            nc.vector.tensor_reduce(out=total[:], in_=weighted[:], axis=AXIS.X, op=ALU.add)
            inv_total = stats.tile([P, 1], F32)
            nc.vector.reciprocal(out=inv_total[:], in_=total[:])
            row_chunk_scale = stats.tile([P, CHUNKS], F32)
            nc.vector.tensor_scalar(
                out=row_chunk_scale[:], in0=factor[:], scalar1=inv_total[:, 0:1], scalar2=None, op0=ALU.mult
            )
            chunk_scale[b] = row_chunk_scale

        weights = {}
        turned = {}
        weight_grouped = {}
        weight_codes = {}
        weight_scales = {}
        acc = {}

        def normalise(stage, k, on_scalar):
            b, j = divmod(k, CHUNKS)
            chunk_weights = stage.tile([P, CHUNK], BF16)
            if on_scalar:
                nc.scalar.activation(
                    out=chunk_weights[:], in_=exps[k][:], func=ACT.Copy, scale=chunk_scale[b][:, j : j + 1]
                )
            else:
                nc.vector.tensor_scalar(
                    out=chunk_weights[:],
                    in0=exps[k][:],
                    scalar1=chunk_scale[b][:, j : j + 1],
                    scalar2=None,
                    op0=ALU.mult,
                )
            weights[k] = chunk_weights

        def turn(k):
            words = weights[k][:].bitcast(F32)
            turned[k] = []
            for half in range(CHUNK_PASSES // BANK_PASSES):
                turned_bank = psum_turn.tile([P, BANK_PASSES, 2, P], F32, tag="turn_bank")
                for c in range(BANK_PASSES):
                    for u in range(2):
                        first = ((BANK_PASSES * half + c) * 2 + u) * P
                        nc.tensor.transpose(
                            turned_bank[:, c, u, :], words[:, first : first + P], identity[:]
                        )
                turned[k].append(turned_bank)

        def regroup(stage, k):
            chunk_grouped = stage.tile([P, CHUNK_PASSES, P, PACK], BF16, align_bytes=64)
            grouped_words = chunk_grouped[:].bitcast(F32)
            for half in range(CHUNK_PASSES // BANK_PASSES):
                nc.scalar.copy(
                    out=grouped_words[:, BANK_PASSES * half : BANK_PASSES * (half + 1), :, :],
                    in_=turned[k][half][:].rearrange("p c u s -> p c s u"),
                )
            weight_grouped[k] = chunk_grouped

        def quantise(stage, k):
            chunk_codes = stage.tile([P, CHUNK_PASSES * P], U32, align_bytes=64)
            chunk_planes = stage.tile([P, CHUNK_PASSES * P], U8, align_bytes=64)
            nc.vector.quantize_mx(
                out=chunk_codes[:].bitcast(FP8X4),
                scales=chunk_planes[:],
                in_=weight_grouped[k][:].rearrange("p c s t -> p (c s t)"),
            )
            weight_codes[k] = chunk_codes
            weight_scales[k] = chunk_planes

        def multiply(k):
            b, j = divmod(k, CHUNKS)
            if j == 0:
                row_acc = psum_out.tile([P, DIM], F32)
                acc[b] = row_acc
            for c in range(CHUNK_PASSES):
                g = j * CHUNK_PASSES + c
                tokens = slice(c * P, (c + 1) * P)
                nc.tensor.matmul_mx(
                    out=acc[b][:],
                    lhsT=weight_codes[k][:, tokens].bitcast(FP8X4),
                    lhsT_scale=weight_scales[k][:, tokens],
                    rhs=table_codes[:, g, :].bitcast(FP8X4),
                    rhs_scale=table_plane(g),
                    start=(g == 0),
                    stop=(g == PASSES - 1),
                )

        def store(stage, b):
            result = stage.tile([P, DIM], F32)
            nc.scalar.copy(out=result[:], in_=acc[b][:])
            nc.sync.dma_start(out=out[b], in_=result[:])


        with tc.tile_pool(name="table_stage", bufs=1) as table_stage:
            for g in range(TABLE_AHEAD):
                load_table(table_stage, g)
            for k in range(CHUNKS):
                spread_next = k + 1 < CHUNKS and (k + 1) % TENSOR_EVERY != 0
                for quarter in range(CHUNK_PASSES):
                    g = k * CHUNK_PASSES + quarter
                    if g + TABLE_AHEAD < PASSES:
                        load_table(table_stage, g + TABLE_AHEAD)
                    regroup_table(table_stage, g)
                    if g >= TABLE_LAG:
                        quantise_table(g - TABLE_LAG)
                    if quarter == 0:
                        logits(k)
                        if k >= 1:
                            exponentials(k - 1)
                    if quarter == 1:
                        maximum(k)
                    if quarter < 2 and spread_next:
                        spread_projection(k + 1, quarter)
                    if quarter >= 2 and spread_next:
                        collect_projection(k + 1, quarter - 2)
            for g in range(PASSES - TABLE_LAG, PASSES):
                quantise_table(g)

        with tc.tile_pool(name="weight_stage", bufs=2, reuse_waits="tile") as weight_stage:
            for k in range(CHUNKS, TOTAL + MULTIPLY_LAG):
                row_ends = k % CHUNKS == 0 and k <= TOTAL
                if row_ends:
                    row_top(k // CHUNKS - 1)
                if k < TOTAL:
                    logits(k)
                    maximum(k)
                on_scalar = k < TOTAL and k % 2 == 1
                if k - NORMALISE_LAG < TOTAL and on_scalar:
                    normalise(weight_stage, k - NORMALISE_LAG, True)
                    turn(k - NORMALISE_LAG)
                if k - 1 < TOTAL:
                    exponentials(k - 1)
                if row_ends:
                    row_scales(k // CHUNKS - 1)
                if k - NORMALISE_LAG < TOTAL and not on_scalar:
                    normalise(weight_stage, k - NORMALISE_LAG, False)
                    turn(k - NORMALISE_LAG)
                if 0 <= k - REGROUP_LAG < TOTAL:
                    regroup(weight_stage, k - REGROUP_LAG)
                if 0 <= k - MULTIPLY_LAG:
                    quantise(weight_stage, k - MULTIPLY_LAG)
                    multiply(k - MULTIPLY_LAG)
                    if (k - MULTIPLY_LAG) % CHUNKS == CHUNKS - 1:
                        store(weight_stage, (k - MULTIPLY_LAG) // CHUNKS)
